import numpy as np
import ml_dtypes


def mxq(x, axis, fmt="e4m3"):
    dtype, down = {"e4m3": (ml_dtypes.float8_e4m3fn, 7), "e5m2": (ml_dtypes.float8_e5m2, 14)}[fmt]
    v = np.moveaxis(np.asarray(x, np.float32).astype(ml_dtypes.bfloat16).astype(np.float64), axis, -1)
    blocks = v.reshape(v.shape[:-1] + (-1, 32))
    amax = np.abs(blocks).max(-1, keepdims=True)
    byte = np.maximum(np.where(amax > 0, np.frexp(amax)[1] - 1 + 127, 0) - down, 1)
    scale = np.exp2(byte - 127.0)
    codes = (blocks / scale).astype(np.float32).astype(dtype).astype(np.float64)
    return np.moveaxis((codes * scale).reshape(v.shape), -1, axis)


WIDE = False


def mx_kscale(k):
    if not WIDE:
        return np.ones(k)
    levels = np.array([10, -10, 5, -5, 0])
    a = np.random.permutation(np.resize(levels, k // 512 * 4)).reshape(k // 512, 4)
    idx = np.arange(k)
    return np.exp2(a[idx // 512, idx % 128 // 32])


BF16 = ml_dtypes.bfloat16


def bf(x):
    return np.asarray(x, np.float32).astype(BF16)


def f64(x):
    return np.asarray(x).astype(np.float64)


E2M1 = np.array([0.0, 0.5, 1.0, 1.5, 2.0, 3.0, 4.0, 6.0, -0.0, -0.5, -1.0, -1.5, -2.0, -3.0, -4.0, -6.0])


def pack_weight(w, fmt):
    k, n = w.shape
    w = f64(bf(w)).reshape(k // 32, 32, n)
    amax = np.abs(w).max(1)
    if fmt == "e4m3":
        byte = np.frexp(amax)[1] - 1 + 127 - 7
    else:
        mant, ex = np.frexp(amax / 6.0)
        byte = np.where(mant > 0.5, ex, ex - 1) + 127
    byte = np.clip(np.where(amax > 0, byte, 1), 1, 254)
    scaled = (w * np.exp2(127.0 - byte)[:, None, :]).reshape(k, n).astype(np.float32)
    by_word = np.ascontiguousarray(scaled.reshape(k // 512, 128, 4, n).transpose(0, 1, 3, 2))
    if fmt == "e4m3":
        words = by_word.astype(ml_dtypes.float8_e4m3fn).view(np.uint8)
    else:
        c = by_word.astype(ml_dtypes.float4_e2m1fn).view(np.uint8) & 0xF
        words = c[..., 0::2] | (c[..., 1::2] << 4)
    return np.ascontiguousarray(words), np.ascontiguousarray(byte.astype(np.uint8).reshape(k // 512, 16, n))


def unpack_weight(words, scales, fmt):
    g, p, n, _ = words.shape
    if fmt == "e4m3":
        vals = np.ascontiguousarray(words).view(ml_dtypes.float8_e4m3fn).astype(np.float64)
    else:
        nib = np.empty((g, p, n, 4), np.uint8)
        nib[..., 0::2] = words & 0xF
        nib[..., 1::2] = words >> 4
        vals = E2M1[nib]
    vals = vals * np.repeat(np.exp2(scales.astype(np.float64) - 127.0), 8, axis=1)[..., None]
    return vals.transpose(0, 1, 3, 2).reshape(g * 512, n)


B, I, O, G = 512, 512, 512, 32


def setup_inputs():
    s = mx_kscale(I * G).reshape(I, G)[:, 0]
    a = np.log2(s / s.max())
    d = np.sqrt(np.abs(a) * np.log(2.0) / 20.0)
    u = np.random.random((B, I))
    x = np.where(a < 0, 1.0 + d + 0.1 * (u - 0.5), u)
    w = np.random.standard_normal((I * G, O)) * 2.0 / np.sqrt(I * G) * np.repeat(np.exp2(-a), G)[:, None]
    words, scales = pack_weight(w, "e4m3")
    return {"x": bf(x), "spline_weight_words": words, "spline_weight_scales": scales,
            "base_weight": bf(np.random.standard_normal((O, I)) / np.sqrt(I)),
            "grid": bf(np.linspace(0.0, 1.0, G))}


def reference(x, spline_weight_words, spline_weight_scales, base_weight, grid):
    x = f64(x)
    base_output = x @ f64(base_weight).T
    basis = np.exp(-20.0 * (x[:, :, None] - f64(grid)[None, None, :]) ** 2)
    basis = basis.reshape(x.shape[0], -1)
    return base_output + (mxq(basis, 1, "e4m3") @ unpack_weight(spline_weight_words, spline_weight_scales, "e4m3"))

@@ -1,0 +1,235 @@
+from contextlib import ExitStack
+
+import concourse.mybir as mybir
+from concourse.masks import make_identity
+
+F32 = mybir.dt.float32
+BF16 = mybir.dt.bfloat16
+I32 = mybir.dt.int32
+U32 = mybir.dt.uint32
+U8 = mybir.dt.uint8
+FP8X4 = mybir.dt.float8_e4m3fn_x4
+ACT = mybir.ActivationFunctionType
+ALU = mybir.AluOpType
+AXIS_X = mybir.AxisListType.X
+
+P = 128
+BATCH = 512
+FEATURES = 512
+OUTPUTS = 512
+GRID = 32
+SHARPNESS = 20.0
+
+PACK = 4
+K_PASS = P * PACK
+PASSES = FEATURES * GRID // K_PASS
+FEATURES_PER_PASS = K_PASS // GRID
+COPIES = P // FEATURES_PER_PASS
+PASSES_PER_TILE = P // FEATURES_PER_PASS
+TILES = 4
+VECTOR_PLANES = 3
+RUN = 4
+W_CHUNK = 4
+
+FLOPS = 2 * BATCH * FEATURES * GRID * OUTPUTS + 2 * BATCH * FEATURES * OUTPUTS
+
+
+def tile_rbfkanlayer_kernel(
+    tc, x, spline_weight_words, spline_weight_scales, base_weight, grid, out
+):
+    nc = tc.nc
+    with ExitStack() as ctx:
+        ctx.enter_context(tc.manual_schedule())
+        keep = ctx.enter_context(tc.tile_pool(name="keep", bufs=1))
+        work = ctx.enter_context(tc.tile_pool(name="work", bufs=3))
+        psum_acc = ctx.enter_context(tc.psum_pool(name="psum_acc", bufs=1))
+        psum_tmp = ctx.enter_context(tc.psum_pool(name="psum_tmp", bufs=4))
+
+        x_rows = keep.tile([P, TILES, FEATURES], BF16)
+        x_view = x.rearrange("(n p) i -> p n i", p=P)
+        grid_all = keep.tile([P, GRID], BF16)
+        for it in range(TILES):
+            cols = slice(it * P, (it + 1) * P)
+            nc.sync.dma_start(out=x_rows[:, :, cols], in_=x_view[:, :, cols])
+            if it == 0:
+                nc.sync.dma_start(out=grid_all[:], in_=grid.partition_broadcast(P))
+        w_rows = keep.tile([P, TILES, FEATURES], BF16)
+        nc.scalar.dma_start(out=w_rows[:], in_=base_weight.rearrange("(n p) i -> p n i", p=P))
+
+        w_scales = keep.tile([P, PASSES, OUTPUTS], U8, align_bytes=64)
+        nc.vector.memset(w_scales[:].rearrange("p g n -> p (g n)").bitcast(I32), 0)
+        for quad in range(4):
+            nc.sync.dma_start(
+                out=w_scales[32 * quad : 32 * quad + 4, :, :].bitcast(I32),
+                in_=spline_weight_scales[:, 4 * quad : 4 * quad + 4, :]
+                .rearrange("g r n -> r g n")
+                .bitcast(I32),
+            )
+        w_words = keep.tile([P, PASSES, PACK * OUTPUTS], U8, align_bytes=64)
+        for first in range(0, PASSES, W_CHUNK):
+            chunk = slice(first, first + W_CHUNK)
+            nc.sync.dma_start(
+                out=w_words[:, chunk, :].bitcast(I32),
+                in_=spline_weight_words[chunk].rearrange("g p n t -> p g (n t)").bitcast(I32),
+            )
+
+        warm = keep.tile([P, 1], F32)
+        nc.gpsimd.memset(warm[:], 0.0)
+        nc.scalar.activation(out=warm[:], in_=warm[:], func=ACT.Exp)
+
+        ident = keep.tile([P, P], BF16)
+        make_identity(nc, ident[:])
+        spread = keep.tile([P, COPIES * P], BF16)
+        nc.vector.tensor_copy(
+            out=spread[:].rearrange("j (c r) -> j c r", r=COPIES),
+            in_=ident[:].unsqueeze(2).to_broadcast([P, P, COPIES]),
+        )
+        own = keep.tile([P, COPIES], F32)
+        nc.vector.tensor_reduce(
+            out=own[:], in_=ident[:].rearrange("p (a q) -> p q a", q=COPIES), axis=AXIS_X, op=ALU.add
+        )
+        picked = keep.tile([P, PACK, COPIES], F32)
+        nc.vector.tensor_tensor(
+            out=picked[:],
+            in0=grid_all[:].rearrange("p (q t) -> p t q", t=PACK),
+            in1=own[:].unsqueeze(1).to_broadcast([P, PACK, COPIES]),
+            op=ALU.mult,
+        )
+        centre = keep.tile([P, PACK], F32)
+        nc.vector.tensor_reduce(out=centre[:], in_=picked[:], axis=AXIS_X, op=ALU.add)
+        neg_centre = keep.tile([P, PACK], F32)
+        nc.vector.tensor_scalar(
+            out=neg_centre[:], in0=centre[:], scalar1=-1.0, scalar2=None, op0=ALU.mult
+        )
+
+        xT = keep.tile([P, TILES, BATCH], BF16)
+        wT = keep.tile([P, TILES, OUTPUTS], BF16)
+        base = keep.tile([P, TILES, OUTPUTS], F32)
+
+        def turn(rows, it):
+            turned = psum_tmp.tile([P, TILES * P], BF16, tag="tmp")
+            for n in range(TILES):
+                nc.tensor.transpose(
+                    turned[:, n * P : (n + 1) * P], rows[:, n, it * P : (it + 1) * P], ident[:]
+                )
+            return turned
+
+        def base_product(bt):
+            product = psum_tmp.tile([P, OUTPUTS], F32, tag="tmp")
+            for it in range(TILES):
+                nc.tensor.matmul(
+                    out=product[:],
+                    lhsT=xT[:, it, bt * P : (bt + 1) * P],
+                    rhs=wT[:, it, :],
+                    start=(it == 0),
+                    stop=(it == TILES - 1),
+                )
+            return product
+
+        def side_step(kind, index):
+            if kind == "x":
+                return turn(x_rows, index), xT[:, index, :]
+            if kind == "w":
+                return turn(w_rows, index), wT[:, index, :]
+            return base_product(index), base[:, index, :]
+
+        side_steps = (
+            [("x", it) for it in range(1, TILES)]
+            + [("w", it) for it in range(TILES)]
+            + [("base", bt) for bt in range(TILES)]
+        )
+
+        acc = [psum_acc.tile([P, OUTPUTS], F32, name="acc%d" % bt) for bt in range(TILES)]
+        x_banks = {}
+        squares = {}
+        bases = {}
+
+        def spread_x(g):
+            x_bank = psum_tmp.tile([P, BATCH], BF16, tag="tmp")
+            q = g % PASSES_PER_TILE
+            nc.tensor.matmul(
+                out=x_bank[:],
+                lhsT=spread[:, q * P : (q + 1) * P],
+                rhs=xT[:, g // PASSES_PER_TILE, :],
+                start=True,
+                stop=True,
+            )
+            x_banks[g] = x_bank
+
+        def square_distances(g):
+            x_bank = x_banks[g]
+            x_copy = work.tile([P, BATCH], BF16)
+            nc.scalar.copy(out=x_copy[:], in_=x_bank[:])
+            square = work.tile([P, PACK, BATCH], F32)
+            for t in range(VECTOR_PLANES, PACK):
+                nc.scalar.activation(
+                    out=square[:, t, :], in_=x_bank[:], func=ACT.Square, bias=neg_centre[:, t : t + 1]
+                )
+            distance = work.tile([P, VECTOR_PLANES, BATCH], F32)
+            for t in range(VECTOR_PLANES):
+                nc.vector.tensor_scalar(
+                    out=distance[:, t, :],
+                    in0=x_copy[:],
+                    scalar1=centre[:, t : t + 1],
+                    scalar2=None,
+                    op0=ALU.subtract,
+                )
+            nc.vector.tensor_tensor(
+                out=square[:, 0:VECTOR_PLANES, :], in0=distance[:], in1=distance[:], op=ALU.mult
+            )
+            squares[g] = square
+
+        def exponentials(g):
+            square = squares[g]
+            basis = work.tile([P, BATCH, PACK], BF16, align_bytes=64)
+            nc.scalar.activation(
+                out=basis[:].rearrange("p (c i) t -> p c t i", i=RUN),
+                in_=square[:].rearrange("p t (c i) -> p c t i", i=RUN),
+                func=ACT.Exp,
+                scale=-SHARPNESS,
+            )
+            bases[g] = basis
+
+        def quantise_and_multiply(g):
+            basis = bases[g]
+            codes = work.tile([P, BATCH], U32, align_bytes=64)
+            scales = work.tile([P, BATCH], U8, align_bytes=64)
+            nc.vector.quantize_mx(
+                out=codes[:].bitcast(FP8X4),
+                scales=scales[:],
+                in_=basis[:].rearrange("p b t -> p (b t)"),
+            )
+            for bt in range(TILES):
+                rows = slice(bt * P, (bt + 1) * P)
+                nc.tensor.matmul_mx(
+                    out=acc[bt][:],
+                    lhsT=codes[:, rows].bitcast(FP8X4),
+                    lhsT_scale=scales[:, rows],
+                    rhs=w_words[:, g, :].bitcast(FP8X4),
+                    rhs_scale=w_scales[:, g, :],
+                    start=(g == 0),
+                    stop=(g == PASSES - 1),
+                )
+
+        first_features = turn(x_rows, 0)
+        nc.scalar.copy(out=xT[:, 0, :], in_=first_features[:])
+        spread_x(0)
+        spread_x(1)
+        square_distances(0)
+        for g in range(PASSES):
+            side = side_step(*side_steps[g]) if g < len(side_steps) else None
+            if g + 2 < PASSES:
+                spread_x(g + 2)
+            if g + 1 < PASSES:
+                square_distances(g + 1)
+            exponentials(g)
+            if side is not None:
+                nc.scalar.copy(out=side[1], in_=side[0][:])
+            if g >= 1:
+                quantise_and_multiply(g - 1)
+        quantise_and_multiply(PASSES - 1)
+
+        for bt in range(TILES):
+            result = work.tile([P, OUTPUTS], F32)
+            nc.vector.tensor_tensor(out=result[:], in0=acc[bt][:], in1=base[:, bt, :], op=ALU.add)
+            nc.sync.dma_start(out=out[bt * P : (bt + 1) * P, :], in_=result[:])

@@ -30,6 +30,8 @@ TILES = 4
 VECTOR_PLANES = 3
 RUN = 4
 W_CHUNK = 4
+SPREAD_AHEAD = 4
+COPY_AHEAD = 3
 
 FLOPS = 2 * BATCH * FEATURES * GRID * OUTPUTS + 2 * BATCH * FEATURES * OUTPUTS
 
@@ -42,6 +44,7 @@ def tile_rbfkanlayer_kernel(
         ctx.enter_context(tc.manual_schedule())
         keep = ctx.enter_context(tc.tile_pool(name="keep", bufs=1))
         work = ctx.enter_context(tc.tile_pool(name="work", bufs=3))
+        ahead = ctx.enter_context(tc.tile_pool(name="ahead", bufs=COPY_AHEAD + 1))
         psum_acc = ctx.enter_context(tc.psum_pool(name="psum_acc", bufs=1))
         psum_tmp = ctx.enter_context(tc.psum_pool(name="psum_tmp", bufs=4))
 
@@ -141,7 +144,9 @@ def tile_rbfkanlayer_kernel(
 
         acc = [psum_acc.tile([P, OUTPUTS], F32, name="acc%d" % bt) for bt in range(TILES)]
         x_banks = {}
+        x_copies = {}
         squares = {}
+        gaps = {}
         bases = {}
 
         def spread_x(g):
@@ -156,28 +161,36 @@ def tile_rbfkanlayer_kernel(
             )
             x_banks[g] = x_bank
 
-        def square_distances(g):
-            x_bank = x_banks[g]
-            x_copy = work.tile([P, BATCH], BF16)
-            nc.scalar.copy(out=x_copy[:], in_=x_bank[:])
+        def copy_x(g):
+            x_copy = ahead.tile([P, BATCH], BF16)
+            nc.scalar.copy(out=x_copy[:], in_=x_banks[g][:])
+            x_copies[g] = x_copy
+
+        def distances(g):
             square = work.tile([P, PACK, BATCH], F32)
             for t in range(VECTOR_PLANES, PACK):
                 nc.scalar.activation(
-                    out=square[:, t, :], in_=x_bank[:], func=ACT.Square, bias=neg_centre[:, t : t + 1]
+                    out=square[:, t, :],
+                    in_=x_copies[g][:],
+                    func=ACT.Square,
+                    bias=neg_centre[:, t : t + 1],
                 )
             distance = work.tile([P, VECTOR_PLANES, BATCH], F32)
             for t in range(VECTOR_PLANES):
                 nc.vector.tensor_scalar(
                     out=distance[:, t, :],
-                    in0=x_copy[:],
+                    in0=x_copies[g][:],
                     scalar1=centre[:, t : t + 1],
                     scalar2=None,
                     op0=ALU.subtract,
                 )
-            nc.vector.tensor_tensor(
-                out=square[:, 0:VECTOR_PLANES, :], in0=distance[:], in1=distance[:], op=ALU.mult
-            )
             squares[g] = square
+            gaps[g] = distance
+
+        def square_distances(g):
+            nc.vector.tensor_tensor(
+                out=squares[g][:, 0:VECTOR_PLANES, :], in0=gaps[g][:], in1=gaps[g][:], op=ALU.mult
+            )
 
         def exponentials(g):
             square = squares[g]
@@ -191,6 +204,8 @@ def tile_rbfkanlayer_kernel(
             bases[g] = basis
 
         def quantise_and_multiply(g):
+            if g < 0:
+                return
             basis = bases[g]
             codes = work.tile([P, BATCH], U32, align_bytes=64)
             scales = work.tile([P, BATCH], U8, align_bytes=64)
@@ -213,20 +228,26 @@ def tile_rbfkanlayer_kernel(
 
         first_features = turn(x_rows, 0)
         nc.scalar.copy(out=xT[:, 0, :], in_=first_features[:])
-        spread_x(0)
-        spread_x(1)
+        for g in range(SPREAD_AHEAD):
+            spread_x(g)
+        for g in range(COPY_AHEAD):
+            copy_x(g)
+        distances(0)
         square_distances(0)
         for g in range(PASSES):
             side = side_step(*side_steps[g]) if g < len(side_steps) else None
-            if g + 2 < PASSES:
-                spread_x(g + 2)
+            if g + SPREAD_AHEAD < PASSES:
+                spread_x(g + SPREAD_AHEAD)
+            if g + COPY_AHEAD < PASSES:
+                copy_x(g + COPY_AHEAD)
             if g + 1 < PASSES:
-                square_distances(g + 1)
+                distances(g + 1)
             exponentials(g)
             if side is not None:
                 nc.scalar.copy(out=side[1], in_=side[0][:])
-            if g >= 1:
-                quantise_and_multiply(g - 1)
+            quantise_and_multiply(g - 1)
+            if g + 1 < PASSES:
+                square_distances(g + 1)
         quantise_and_multiply(PASSES - 1)
 
         for bt in range(TILES):

@@ -27,11 +27,12 @@ FEATURES_PER_PASS = K_PASS // GRID
 COPIES = P // FEATURES_PER_PASS
 PASSES_PER_TILE = P // FEATURES_PER_PASS
 TILES = 4
+ROUND = 2
+ROUNDS = PASSES // ROUND
+COLS = ROUND * BATCH
 VECTOR_PLANES = 3
 RUN = 4
 W_CHUNK = 4
-SPREAD_AHEAD = 4
-COPY_AHEAD = 3
 
 FLOPS = 2 * BATCH * FEATURES * GRID * OUTPUTS + 2 * BATCH * FEATURES * OUTPUTS
 
@@ -43,10 +44,11 @@ def tile_rbfkanlayer_kernel(
     with ExitStack() as ctx:
         ctx.enter_context(tc.manual_schedule())
         keep = ctx.enter_context(tc.tile_pool(name="keep", bufs=1))
-        work = ctx.enter_context(tc.tile_pool(name="work", bufs=3))
-        ahead = ctx.enter_context(tc.tile_pool(name="ahead", bufs=COPY_AHEAD + 1))
+        work = ctx.enter_context(tc.tile_pool(name="work", bufs=2))
+        ahead = ctx.enter_context(tc.tile_pool(name="ahead", bufs=3))
         psum_acc = ctx.enter_context(tc.psum_pool(name="psum_acc", bufs=1))
-        psum_tmp = ctx.enter_context(tc.psum_pool(name="psum_tmp", bufs=4))
+        psum_x = ctx.enter_context(tc.psum_pool(name="psum_x", bufs=3))
+        psum_side = ctx.enter_context(tc.psum_pool(name="psum_side", bufs=1))
 
         x_rows = keep.tile([P, TILES, FEATURES], BF16)
         x_view = x.rearrange("(n p) i -> p n i", p=P)
@@ -110,7 +112,7 @@ def tile_rbfkanlayer_kernel(
         base = keep.tile([P, TILES, OUTPUTS], F32)
 
         def turn(rows, it):
-            turned = psum_tmp.tile([P, TILES * P], BF16, tag="tmp")
+            turned = psum_side.tile([P, TILES * P], BF16, tag="side")
             for n in range(TILES):
                 nc.tensor.transpose(
                     turned[:, n * P : (n + 1) * P], rows[:, n, it * P : (it + 1) * P], ident[:]
@@ -118,7 +120,7 @@ def tile_rbfkanlayer_kernel(
             return turned
 
         def base_product(bt):
-            product = psum_tmp.tile([P, OUTPUTS], F32, tag="tmp")
+            product = psum_side.tile([P, OUTPUTS], F32, tag="side")
             for it in range(TILES):
                 nc.tensor.matmul(
                     out=product[:],
@@ -145,112 +147,122 @@ def tile_rbfkanlayer_kernel(
         acc = [psum_acc.tile([P, OUTPUTS], F32, name="acc%d" % bt) for bt in range(TILES)]
         x_banks = {}
         x_copies = {}
-        squares = {}
         gaps = {}
+        squares = {}
         bases = {}
 
-        def spread_x(g):
-            x_bank = psum_tmp.tile([P, BATCH], BF16, tag="tmp")
-            q = g % PASSES_PER_TILE
-            nc.tensor.matmul(
-                out=x_bank[:],
-                lhsT=spread[:, q * P : (q + 1) * P],
-                rhs=xT[:, g // PASSES_PER_TILE, :],
-                start=True,
-                stop=True,
-            )
-            x_banks[g] = x_bank
+        def spread_x(u):
+            if u >= ROUNDS:
+                return
+            x_bank = psum_x.tile([P, COLS], BF16)
+            for h in range(ROUND):
+                g = ROUND * u + h
+                q = g % PASSES_PER_TILE
+                nc.tensor.matmul(
+                    out=x_bank[:, h * BATCH : (h + 1) * BATCH],
+                    lhsT=spread[:, q * P : (q + 1) * P],
+                    rhs=xT[:, g // PASSES_PER_TILE, :],
+                    start=True,
+                    stop=True,
+                )
+            x_banks[u] = x_bank
 
-        def copy_x(g):
-            x_copy = ahead.tile([P, BATCH], BF16)
-            nc.scalar.copy(out=x_copy[:], in_=x_banks[g][:])
-            x_copies[g] = x_copy
+        def distances(u):
+            if u >= ROUNDS:
+                return
+            x_copy = ahead.tile([P, COLS], BF16)
+            nc.vector.tensor_copy(out=x_copy[:], in_=x_banks[u][:])
+            distance = work.tile([P, VECTOR_PLANES, COLS], F32)
+            for t in range(VECTOR_PLANES):
+                nc.gpsimd.tensor_scalar(
+                    out=distance[:, t, :],
+                    in0=x_copy[:],
+                    scalar1=neg_centre[:, t : t + 1],
+                    scalar2=1.0,
+                    op0=ALU.add,
+                    op1=ALU.mult,
+                )
+            x_copies[u] = x_copy
+            gaps[u] = distance
 
-        def distances(g):
-            square = work.tile([P, PACK, BATCH], F32)
+        def square_distances(u):
+            if u >= ROUNDS:
+                return
+            square = work.tile([P, PACK, COLS], F32)
+            for t in range(VECTOR_PLANES):
+                nc.vector.scalar_tensor_tensor(
+                    out=square[:, t, :],
+                    in0=x_banks[u][:],
+                    scalar=centre[:, t : t + 1],
+                    in1=gaps[u][:, t, :],
+                    op0=ALU.subtract,
+                    op1=ALU.mult,
+                )
             for t in range(VECTOR_PLANES, PACK):
                 nc.scalar.activation(
                     out=square[:, t, :],
-                    in_=x_copies[g][:],
+                    in_=x_copies[u][:],
                     func=ACT.Square,
                     bias=neg_centre[:, t : t + 1],
                 )
-            distance = work.tile([P, VECTOR_PLANES, BATCH], F32)
-            for t in range(VECTOR_PLANES):
-                nc.vector.tensor_scalar(
-                    out=distance[:, t, :],
-                    in0=x_copies[g][:],
-                    scalar1=centre[:, t : t + 1],
-                    scalar2=None,
-                    op0=ALU.subtract,
+            squares[u] = square
+
+        def exponentials(u):
+            basis = work.tile([P, COLS, PACK], BF16, align_bytes=64)
+            for h in range(ROUND):
+                cols = slice(h * BATCH, (h + 1) * BATCH)
+                nc.scalar.activation(
+                    out=basis[:, cols, :].rearrange("p (c i) t -> p c t i", i=RUN),
+                    in_=squares[u][:, :, cols].rearrange("p t (c i) -> p c t i", i=RUN),
+                    func=ACT.Exp,
+                    scale=-SHARPNESS,
                 )
-            squares[g] = square
-            gaps[g] = distance
+            bases[u] = basis
 
-        def square_distances(g):
-            nc.vector.tensor_tensor(
-                out=squares[g][:, 0:VECTOR_PLANES, :], in0=gaps[g][:], in1=gaps[g][:], op=ALU.mult
-            )
-
-        def exponentials(g):
-            square = squares[g]
-            basis = work.tile([P, BATCH, PACK], BF16, align_bytes=64)
-            nc.scalar.activation(
-                out=basis[:].rearrange("p (c i) t -> p c t i", i=RUN),
-                in_=square[:].rearrange("p t (c i) -> p c t i", i=RUN),
-                func=ACT.Exp,
-                scale=-SHARPNESS,
-            )
-            bases[g] = basis
-
-        def quantise_and_multiply(g):
-            if g < 0:
+        def quantise_and_multiply(u):
+            if u < 0:
                 return
-            basis = bases[g]
-            codes = work.tile([P, BATCH], U32, align_bytes=64)
-            scales = work.tile([P, BATCH], U8, align_bytes=64)
+            codes = work.tile([P, COLS], U32, align_bytes=64)
+            scales = work.tile([P, COLS], U8, align_bytes=64)
             nc.vector.quantize_mx(
                 out=codes[:].bitcast(FP8X4),
                 scales=scales[:],
-                in_=basis[:].rearrange("p b t -> p (b t)"),
+                in_=bases[u][:].rearrange("p c t -> p (c t)"),
             )
             for bt in range(TILES):
-                rows = slice(bt * P, (bt + 1) * P)
-                nc.tensor.matmul_mx(
-                    out=acc[bt][:],
-                    lhsT=codes[:, rows].bitcast(FP8X4),
-                    lhsT_scale=scales[:, rows],
-                    rhs=w_words[:, g, :].bitcast(FP8X4),
-                    rhs_scale=w_scales[:, g, :],
-                    start=(g == 0),
-                    stop=(g == PASSES - 1),
-                )
+                for h in range(ROUND):
+                    g = ROUND * u + h
+                    rows = slice(h * BATCH + bt * P, h * BATCH + (bt + 1) * P)
+                    nc.tensor.matmul_mx(
+                        out=acc[bt][:],
+                        lhsT=codes[:, rows].bitcast(FP8X4),
+                        lhsT_scale=scales[:, rows],
+                        rhs=w_words[:, g, :].bitcast(FP8X4),
+                        rhs_scale=w_scales[:, g, :],
+                        start=(g == 0),
+                        stop=(g == PASSES - 1),
+                    )
 
         first_features = turn(x_rows, 0)
         nc.scalar.copy(out=xT[:, 0, :], in_=first_features[:])
-        for g in range(SPREAD_AHEAD):
-            spread_x(g)
-        for g in range(COPY_AHEAD):
-            copy_x(g)
+        spread_x(0)
+        spread_x(1)
+        spread_x(2)
         distances(0)
+        distances(1)
         square_distances(0)
-        for g in range(PASSES):
-            side = side_step(*side_steps[g]) if g < len(side_steps) else None
-            if g + SPREAD_AHEAD < PASSES:
-                spread_x(g + SPREAD_AHEAD)
-            if g + COPY_AHEAD < PASSES:
-                copy_x(g + COPY_AHEAD)
-            if g + 1 < PASSES:
-                distances(g + 1)
-            exponentials(g)
+        for u in range(ROUNDS):
+            side = side_step(*side_steps[u]) if u < len(side_steps) else None
+            spread_x(u + 3)
+            quantise_and_multiply(u - 1)
+            distances(u + 2)
+            square_distances(u + 1)
+            exponentials(u)
             if side is not None:
                 nc.scalar.copy(out=side[1], in_=side[0][:])
-            quantise_and_multiply(g - 1)
-            if g + 1 < PASSES:
-                square_distances(g + 1)
-        quantise_and_multiply(PASSES - 1)
+        quantise_and_multiply(ROUNDS - 1)
 
         for bt in range(TILES):
-            result = work.tile([P, OUTPUTS], F32)
+            result = ahead.tile([P, OUTPUTS], F32)
             nc.vector.tensor_tensor(out=result[:], in0=acc[bt][:], in1=base[:, bt, :], op=ALU.add)
             nc.sync.dma_start(out=out[bt * P : (bt + 1) * P, :], in_=result[:])

@@ -30,7 +30,8 @@ TILES = 4
 ROUND = 2
 ROUNDS = PASSES // ROUND
 COLS = ROUND * BATCH
-VECTOR_PLANES = 3
+SCALAR_PLANES = 2
+SCALAR_COLS = 512
 RUN = 4
 W_CHUNK = 4
 
@@ -151,6 +152,12 @@ def tile_rbfkanlayer_kernel(
         squares = {}
         bases = {}
 
+        def in_runs(columns):
+            return columns.rearrange("p (c i) -> p c i", i=RUN)
+
+        def first_vector_column(t):
+            return SCALAR_COLS if t >= PACK - SCALAR_PLANES else 0
+
         def spread_x(u):
             if u >= ROUNDS:
                 return
@@ -172,11 +179,12 @@ def tile_rbfkanlayer_kernel(
                 return
             x_copy = ahead.tile([P, COLS], BF16)
             nc.vector.tensor_copy(out=x_copy[:], in_=x_banks[u][:])
-            distance = work.tile([P, VECTOR_PLANES, COLS], F32)
-            for t in range(VECTOR_PLANES):
+            distance = work.tile([P, PACK, COLS], F32)
+            for t in range(PACK):
+                first = first_vector_column(t)
                 nc.gpsimd.tensor_scalar(
-                    out=distance[:, t, :],
-                    in0=x_copy[:],
+                    out=distance[:, t, first:],
+                    in0=x_copy[:, first:],
                     scalar1=neg_centre[:, t : t + 1],
                     scalar2=1.0,
                     op0=ALU.add,
@@ -188,20 +196,21 @@ def tile_rbfkanlayer_kernel(
         def square_distances(u):
             if u >= ROUNDS:
                 return
-            square = work.tile([P, PACK, COLS], F32)
-            for t in range(VECTOR_PLANES):
+            square = work.tile([P, COLS // RUN, PACK, RUN], F32)
+            for t in range(PACK):
+                first = first_vector_column(t)
                 nc.vector.scalar_tensor_tensor(
-                    out=square[:, t, :],
-                    in0=x_banks[u][:],
+                    out=square[:, first // RUN :, t, :],
+                    in0=in_runs(x_banks[u][:, first:]),
                     scalar=centre[:, t : t + 1],
-                    in1=gaps[u][:, t, :],
+                    in1=in_runs(gaps[u][:, t, first:]),
                     op0=ALU.subtract,
                     op1=ALU.mult,
                 )
-            for t in range(VECTOR_PLANES, PACK):
+            for t in range(PACK - SCALAR_PLANES, PACK):
                 nc.scalar.activation(
-                    out=square[:, t, :],
-                    in_=x_copies[u][:],
+                    out=square[:, : SCALAR_COLS // RUN, t, :],
+                    in_=in_runs(x_copies[u][:, :SCALAR_COLS]),
                     func=ACT.Square,
                     bias=neg_centre[:, t : t + 1],
                 )
@@ -210,38 +219,38 @@ def tile_rbfkanlayer_kernel(
         def exponentials(u):
             basis = work.tile([P, COLS, PACK], BF16, align_bytes=64)
             for h in range(ROUND):
-                cols = slice(h * BATCH, (h + 1) * BATCH)
                 nc.scalar.activation(
-                    out=basis[:, cols, :].rearrange("p (c i) t -> p c t i", i=RUN),
-                    in_=squares[u][:, :, cols].rearrange("p t (c i) -> p c t i", i=RUN),
+                    out=basis[:, h * BATCH : (h + 1) * BATCH, :].rearrange(
+                        "p (c i) t -> p c t i", i=RUN
+                    ),
+                    in_=squares[u][:, h * BATCH // RUN : (h + 1) * BATCH // RUN, :, :],
                     func=ACT.Exp,
                     scale=-SHARPNESS,
                 )
             bases[u] = basis
 
-        def quantise_and_multiply(u):
-            if u < 0:
+        def quantise_and_multiply(g):
+            if g < 0:
                 return
-            codes = work.tile([P, COLS], U32, align_bytes=64)
-            scales = work.tile([P, COLS], U8, align_bytes=64)
+            h = g % ROUND
+            codes = ahead.tile([P, BATCH], U32, align_bytes=64)
+            scales = ahead.tile([P, BATCH], U8, align_bytes=64)
             nc.vector.quantize_mx(
                 out=codes[:].bitcast(FP8X4),
                 scales=scales[:],
-                in_=bases[u][:].rearrange("p c t -> p (c t)"),
+                in_=bases[g // ROUND][:, h * BATCH : (h + 1) * BATCH, :].rearrange("p c t -> p (c t)"),
             )
             for bt in range(TILES):
-                for h in range(ROUND):
-                    g = ROUND * u + h
-                    rows = slice(h * BATCH + bt * P, h * BATCH + (bt + 1) * P)
-                    nc.tensor.matmul_mx(
-                        out=acc[bt][:],
-                        lhsT=codes[:, rows].bitcast(FP8X4),
-                        lhsT_scale=scales[:, rows],
-                        rhs=w_words[:, g, :].bitcast(FP8X4),
-                        rhs_scale=w_scales[:, g, :],
-                        start=(g == 0),
-                        stop=(g == PASSES - 1),
-                    )
+                rows = slice(bt * P, (bt + 1) * P)
+                nc.tensor.matmul_mx(
+                    out=acc[bt][:],
+                    lhsT=codes[:, rows].bitcast(FP8X4),
+                    lhsT_scale=scales[:, rows],
+                    rhs=w_words[:, g, :].bitcast(FP8X4),
+                    rhs_scale=w_scales[:, g, :],
+                    start=(g == 0),
+                    stop=(g == PASSES - 1),
+                )
 
         first_features = turn(x_rows, 0)
         nc.scalar.copy(out=xT[:, 0, :], in_=first_features[:])
@@ -254,13 +263,15 @@ def tile_rbfkanlayer_kernel(
         for u in range(ROUNDS):
             side = side_step(*side_steps[u]) if u < len(side_steps) else None
             spread_x(u + 3)
-            quantise_and_multiply(u - 1)
+            for h in range(ROUND):
+                quantise_and_multiply(ROUND * (u - 1) + h)
             distances(u + 2)
             square_distances(u + 1)
             exponentials(u)
             if side is not None:
-                nc.scalar.copy(out=side[1], in_=side[0][:])
-        quantise_and_multiply(ROUNDS - 1)
+                nc.vector.tensor_copy(out=side[1], in_=side[0][:])
+        for h in range(ROUND):
+            quantise_and_multiply(ROUND * (ROUNDS - 1) + h)
 
         for bt in range(TILES):
             result = ahead.tile([P, OUTPUTS], F32)

@@ -31,7 +31,7 @@ ROUND = 2
 ROUNDS = PASSES // ROUND
 COLS = ROUND * BATCH
 SCALAR_PLANES = 2
-SCALAR_COLS = 512
+SCALAR_COLS = 448
 RUN = 4
 W_CHUNK = 4
 
@@ -46,7 +46,7 @@ def tile_rbfkanlayer_kernel(
         ctx.enter_context(tc.manual_schedule())
         keep = ctx.enter_context(tc.tile_pool(name="keep", bufs=1))
         work = ctx.enter_context(tc.tile_pool(name="work", bufs=2))
-        ahead = ctx.enter_context(tc.tile_pool(name="ahead", bufs=3))
+        ahead = ctx.enter_context(tc.tile_pool(name="ahead", bufs=4))
         psum_acc = ctx.enter_context(tc.psum_pool(name="psum_acc", bufs=1))
         psum_x = ctx.enter_context(tc.psum_pool(name="psum_x", bufs=3))
         psum_side = ctx.enter_context(tc.psum_pool(name="psum_side", bufs=1))
@@ -174,23 +174,29 @@ def tile_rbfkanlayer_kernel(
                 )
             x_banks[u] = x_bank
 
-        def distances(u):
+        def copy_x(u):
             if u >= ROUNDS:
                 return
             x_copy = ahead.tile([P, COLS], BF16)
             nc.vector.tensor_copy(out=x_copy[:], in_=x_banks[u][:])
+            x_copies[u] = x_copy
+
+        def distances(u):
+            if u >= ROUNDS:
+                return
+            go = ahead.tile([P, PACK], F32)
+            nc.vector.tensor_copy(out=go[:], in_=neg_centre[:])
             distance = work.tile([P, PACK, COLS], F32)
             for t in range(PACK):
                 first = first_vector_column(t)
                 nc.gpsimd.tensor_scalar(
                     out=distance[:, t, first:],
-                    in0=x_copy[:, first:],
-                    scalar1=neg_centre[:, t : t + 1],
+                    in0=x_copies[u][:, first:],
+                    scalar1=go[:, t : t + 1],
                     scalar2=1.0,
                     op0=ALU.add,
                     op1=ALU.mult,
                 )
-            x_copies[u] = x_copy
             gaps[u] = distance
 
         def square_distances(u):
@@ -257,9 +263,12 @@ def tile_rbfkanlayer_kernel(
         spread_x(0)
         spread_x(1)
         spread_x(2)
+        copy_x(0)
         distances(0)
+        copy_x(1)
         distances(1)
         square_distances(0)
+        copy_x(2)
         for u in range(ROUNDS):
             side = side_step(*side_steps[u]) if u < len(side_steps) else None
             spread_x(u + 3)
@@ -267,6 +276,7 @@ def tile_rbfkanlayer_kernel(
                 quantise_and_multiply(ROUND * (u - 1) + h)
             distances(u + 2)
             square_distances(u + 1)
+            copy_x(u + 3)
             exponentials(u)
             if side is not None:
                 nc.vector.tensor_copy(out=side[1], in_=side[0][:])

from contextlib import ExitStack

import concourse.mybir as mybir
from concourse.masks import make_identity

F32 = mybir.dt.float32
BF16 = mybir.dt.bfloat16
I32 = mybir.dt.int32
U32 = mybir.dt.uint32
U8 = mybir.dt.uint8
FP8X4 = mybir.dt.float8_e4m3fn_x4
ACT = mybir.ActivationFunctionType
ALU = mybir.AluOpType
AXIS_X = mybir.AxisListType.X

P = 128
BATCH = 512
FEATURES = 512
OUTPUTS = 512
GRID = 32
SHARPNESS = 20.0

PACK = 4
K_PASS = P * PACK
PASSES = FEATURES * GRID // K_PASS
FEATURES_PER_PASS = K_PASS // GRID
COPIES = P // FEATURES_PER_PASS
PASSES_PER_TILE = P // FEATURES_PER_PASS
TILES = 4
ROUND = 2
ROUNDS = PASSES // ROUND
COLS = ROUND * BATCH
SCALAR_PLANES = 2
SCALAR_COLS = 448
RUN = 4
W_CHUNK = 4

FLOPS = 2 * BATCH * FEATURES * GRID * OUTPUTS + 2 * BATCH * FEATURES * OUTPUTS


def tile_rbfkanlayer_kernel(
    tc, x, spline_weight_words, spline_weight_scales, base_weight, grid, out
):
    nc = tc.nc
    with ExitStack() as ctx:
        ctx.enter_context(tc.manual_schedule())
        keep = ctx.enter_context(tc.tile_pool(name="keep", bufs=1))
        work = ctx.enter_context(tc.tile_pool(name="work", bufs=2))
        ahead = ctx.enter_context(tc.tile_pool(name="ahead", bufs=4))
        psum_acc = ctx.enter_context(tc.psum_pool(name="psum_acc", bufs=1))
        psum_x = ctx.enter_context(tc.psum_pool(name="psum_x", bufs=3))
        psum_side = ctx.enter_context(tc.psum_pool(name="psum_side", bufs=1))

        x_rows = keep.tile([P, TILES, FEATURES], BF16)
        x_view = x.rearrange("(n p) i -> p n i", p=P)
        grid_all = keep.tile([P, GRID], BF16)
        for it in range(TILES):
            cols = slice(it * P, (it + 1) * P)
            nc.sync.dma_start(out=x_rows[:, :, cols], in_=x_view[:, :, cols])
            if it == 0:
                nc.sync.dma_start(out=grid_all[:], in_=grid.partition_broadcast(P))
        w_rows = keep.tile([P, TILES, FEATURES], BF16)
        nc.scalar.dma_start(out=w_rows[:], in_=base_weight.rearrange("(n p) i -> p n i", p=P))

        w_scales = keep.tile([P, PASSES, OUTPUTS], U8, align_bytes=64)
        nc.vector.memset(w_scales[:].rearrange("p g n -> p (g n)").bitcast(I32), 0)
        for quad in range(4):
            nc.sync.dma_start(
                out=w_scales[32 * quad : 32 * quad + 4, :, :].bitcast(I32),
                in_=spline_weight_scales[:, 4 * quad : 4 * quad + 4, :]
                .rearrange("g r n -> r g n")
                .bitcast(I32),
            )
        w_words = keep.tile([P, PASSES, PACK * OUTPUTS], U8, align_bytes=64)
        for first in range(0, PASSES, W_CHUNK):
            chunk = slice(first, first + W_CHUNK)
            nc.sync.dma_start(
                out=w_words[:, chunk, :].bitcast(I32),
                in_=spline_weight_words[chunk].rearrange("g p n t -> p g (n t)").bitcast(I32),
            )

        warm = keep.tile([P, 1], F32)
        nc.gpsimd.memset(warm[:], 0.0)
        nc.scalar.activation(out=warm[:], in_=warm[:], func=ACT.Exp)

        ident = keep.tile([P, P], BF16)
        make_identity(nc, ident[:])
        spread = keep.tile([P, COPIES * P], BF16)
        nc.vector.tensor_copy(
            out=spread[:].rearrange("j (c r) -> j c r", r=COPIES),
            in_=ident[:].unsqueeze(2).to_broadcast([P, P, COPIES]),
        )
        own = keep.tile([P, COPIES], F32)
        nc.vector.tensor_reduce(
            out=own[:], in_=ident[:].rearrange("p (a q) -> p q a", q=COPIES), axis=AXIS_X, op=ALU.add
        )
        picked = keep.tile([P, PACK, COPIES], F32)
        nc.vector.tensor_tensor(
            out=picked[:],
            in0=grid_all[:].rearrange("p (q t) -> p t q", t=PACK),
            in1=own[:].unsqueeze(1).to_broadcast([P, PACK, COPIES]),
            op=ALU.mult,
        )
        centre = keep.tile([P, PACK], F32)
        nc.vector.tensor_reduce(out=centre[:], in_=picked[:], axis=AXIS_X, op=ALU.add)
        neg_centre = keep.tile([P, PACK], F32)
        nc.vector.tensor_scalar(
            out=neg_centre[:], in0=centre[:], scalar1=-1.0, scalar2=None, op0=ALU.mult
        )

        xT = keep.tile([P, TILES, BATCH], BF16)
        wT = keep.tile([P, TILES, OUTPUTS], BF16)
        base = keep.tile([P, TILES, OUTPUTS], F32)

        def turn(rows, it):
            turned = psum_side.tile([P, TILES * P], BF16, tag="side")
            for n in range(TILES):
                nc.tensor.transpose(
                    turned[:, n * P : (n + 1) * P], rows[:, n, it * P : (it + 1) * P], ident[:]
                )
            return turned

        def base_product(bt):
            product = psum_side.tile([P, OUTPUTS], F32, tag="side")
            for it in range(TILES):
                nc.tensor.matmul(
                    out=product[:],
                    lhsT=xT[:, it, bt * P : (bt + 1) * P],
                    rhs=wT[:, it, :],
                    start=(it == 0),
                    stop=(it == TILES - 1),
                )
            return product

        def side_step(kind, index):
            if kind == "x":
                return turn(x_rows, index), xT[:, index, :]
            if kind == "w":
                return turn(w_rows, index), wT[:, index, :]
            return base_product(index), base[:, index, :]

        side_steps = (
            [("x", it) for it in range(1, TILES)]
            + [("w", it) for it in range(TILES)]
            + [("base", bt) for bt in range(TILES)]
        )

        acc = [psum_acc.tile([P, OUTPUTS], F32, name="acc%d" % bt) for bt in range(TILES)]
        x_banks = {}
        x_copies = {}
        gaps = {}
        squares = {}
        bases = {}

        def in_runs(columns):
            return columns.rearrange("p (c i) -> p c i", i=RUN)

        def first_vector_column(t):
            return SCALAR_COLS if t >= PACK - SCALAR_PLANES else 0

        def spread_x(u):
            if u >= ROUNDS:
                return
            x_bank = psum_x.tile([P, COLS], BF16)
            for h in range(ROUND):
                g = ROUND * u + h
                q = g % PASSES_PER_TILE
                nc.tensor.matmul(
                    out=x_bank[:, h * BATCH : (h + 1) * BATCH],
                    lhsT=spread[:, q * P : (q + 1) * P],
                    rhs=xT[:, g // PASSES_PER_TILE, :],
                    start=True,
                    stop=True,
                )
            x_banks[u] = x_bank

        def copy_x(u):
            if u >= ROUNDS:
                return
            x_copy = ahead.tile([P, COLS], BF16)
            nc.vector.tensor_copy(out=x_copy[:], in_=x_banks[u][:])
            x_copies[u] = x_copy

        def distances(u):
            if u >= ROUNDS:
                return
            go = ahead.tile([P, PACK], F32)
            nc.vector.tensor_copy(out=go[:], in_=neg_centre[:])
            distance = work.tile([P, PACK, COLS], F32)
            for t in range(PACK):
                first = first_vector_column(t)
                nc.gpsimd.tensor_scalar(
                    out=distance[:, t, first:],
                    in0=x_copies[u][:, first:],
                    scalar1=go[:, t : t + 1],
                    scalar2=1.0,
                    op0=ALU.add,
                    op1=ALU.mult,
                )
            gaps[u] = distance

        def square_distances(u):
            if u >= ROUNDS:
                return
            square = work.tile([P, COLS // RUN, PACK, RUN], F32)
            for t in range(PACK):
                first = first_vector_column(t)
                nc.vector.scalar_tensor_tensor(
                    out=square[:, first // RUN :, t, :],
                    in0=in_runs(x_banks[u][:, first:]),
                    scalar=centre[:, t : t + 1],
                    in1=in_runs(gaps[u][:, t, first:]),
                    op0=ALU.subtract,
                    op1=ALU.mult,
                )
            for t in range(PACK - SCALAR_PLANES, PACK):
                nc.scalar.activation(
                    out=square[:, : SCALAR_COLS // RUN, t, :],
                    in_=in_runs(x_copies[u][:, :SCALAR_COLS]),
                    func=ACT.Square,
                    bias=neg_centre[:, t : t + 1],
                )
            squares[u] = square

        def exponentials(u):
            basis = work.tile([P, COLS, PACK], BF16, align_bytes=64)
            for h in range(ROUND):
                nc.scalar.activation(
                    out=basis[:, h * BATCH : (h + 1) * BATCH, :].rearrange(
                        "p (c i) t -> p c t i", i=RUN
                    ),
                    in_=squares[u][:, h * BATCH // RUN : (h + 1) * BATCH // RUN, :, :],
                    func=ACT.Exp,
                    scale=-SHARPNESS,
                )
            bases[u] = basis

        def quantise_and_multiply(g):
            if g < 0:
                return
            h = g % ROUND
            codes = ahead.tile([P, BATCH], U32, align_bytes=64)
            scales = ahead.tile([P, BATCH], U8, align_bytes=64)
            nc.vector.quantize_mx(
                out=codes[:].bitcast(FP8X4),
                scales=scales[:],
                in_=bases[g // ROUND][:, h * BATCH : (h + 1) * BATCH, :].rearrange("p c t -> p (c t)"),
            )
            for bt in range(TILES):
                rows = slice(bt * P, (bt + 1) * P)
                nc.tensor.matmul_mx(
                    out=acc[bt][:],
                    lhsT=codes[:, rows].bitcast(FP8X4),
                    lhsT_scale=scales[:, rows],
                    rhs=w_words[:, g, :].bitcast(FP8X4),
                    rhs_scale=w_scales[:, g, :],
                    start=(g == 0),
                    stop=(g == PASSES - 1),
                )

        first_features = turn(x_rows, 0)
        nc.scalar.copy(out=xT[:, 0, :], in_=first_features[:])
        spread_x(0)
        spread_x(1)
        spread_x(2)
        copy_x(0)
        distances(0)
        copy_x(1)
        distances(1)
        square_distances(0)
        copy_x(2)
        for u in range(ROUNDS):
            side = side_step(*side_steps[u]) if u < len(side_steps) else None
            spread_x(u + 3)
            for h in range(ROUND):
                quantise_and_multiply(ROUND * (u - 1) + h)
            distances(u + 2)
            square_distances(u + 1)
            copy_x(u + 3)
            exponentials(u)
            if side is not None:
                nc.vector.tensor_copy(out=side[1], in_=side[0][:])
        for h in range(ROUND):
            quantise_and_multiply(ROUND * (ROUNDS - 1) + h)

        for bt in range(TILES):
            result = ahead.tile([P, OUTPUTS], F32)
            nc.vector.tensor_tensor(out=result[:], in0=acc[bt][:], in1=base[:, bt, :], op=ALU.add)
            nc.sync.dma_start(out=out[bt * P : (bt + 1) * P, :], in_=result[:])
